import numpy as np
import ml_dtypes


def mxq(x, axis, fmt="e4m3"):
    dtype, down = {"e4m3": (ml_dtypes.float8_e4m3fn, 7), "e5m2": (ml_dtypes.float8_e5m2, 14)}[fmt]
    v = np.moveaxis(np.asarray(x, np.float32).astype(ml_dtypes.bfloat16).astype(np.float64), axis, -1)
    blocks = v.reshape(v.shape[:-1] + (-1, 32))
    amax = np.abs(blocks).max(-1, keepdims=True)
    byte = np.maximum(np.where(amax > 0, np.frexp(amax)[1] - 1 + 127, 0) - down, 1)
    scale = np.exp2(byte - 127.0)
    codes = (blocks / scale).astype(np.float32).astype(dtype).astype(np.float64)
    return np.moveaxis((codes * scale).reshape(v.shape), -1, axis)


WIDE = False


def mx_kscale(k):
    if not WIDE:
        return np.ones(k)
    levels = np.array([10, -10, 5, -5, 0])
    a = np.random.permutation(np.resize(levels, k // 512 * 4)).reshape(k // 512, 4)
    idx = np.arange(k)
    return np.exp2(a[idx // 512, idx % 128 // 32])


BF16 = ml_dtypes.bfloat16


def bf(x):
    return np.asarray(x, np.float32).astype(BF16)


def f64(x):
    return np.asarray(x).astype(np.float64)


B, N, D, R = 1, 2048, 1024, 4
M = N // R


def merge(t, r):
    b, n, d = t.shape
    return t.reshape(b, n // r, r, d).mean(axis=2)


def setup_inputs():
    s, t = mx_kscale(D), mx_kscale(D)
    a = 2.0 / np.sqrt(D)
    return {"x": bf(np.random.standard_normal((B, N, D)) * s),
            "Wq": bf(np.random.standard_normal((D, D)) * a * t[:, None] / s),
            "bq": bf(np.random.standard_normal(D) * 0.5 * t),
            "Wk": bf(np.random.standard_normal((D, D)) * a / t[:, None] / s),
            "bk": bf(np.random.standard_normal(D) * 0.3 / t)}


def reference(x, Wq, bq, Wk, bk):
    xq = mxq(f64(x), 2, "e4m3")
    Q = (xq @ mxq(f64(Wq), 1, "e4m3").T) + f64(bq)
    K = (xq @ mxq(f64(Wk), 1, "e4m3").T) + f64(bk)
    K_m = merge(K, R)
    scores = (mxq(Q, 2, "e4m3") @ mxq(K_m, 2, "e4m3").transpose(0, 2, 1)) * (1.0 / np.sqrt(D))
    return scores + np.log(R)

@@ -1,0 +1,228 @@
+import math
+from contextlib import ExitStack
+
+import concourse.masks as masks
+import concourse.mybir as mybir
+
+BF16 = mybir.dt.bfloat16
+F32 = mybir.dt.float32
+U32 = mybir.dt.uint32
+U8 = mybir.dt.uint8
+FP8X4 = mybir.dt.float8_e4m3fn_x4
+ACT = mybir.ActivationFunctionType
+ALU = mybir.AluOpType
+
+P = 128
+PACK = 4
+K_PASS = P * PACK
+TOKENS = 2048
+FEATURES = 1024
+WINDOW = 4
+KEYS = TOKENS // WINDOW
+PASSES = FEATURES // K_PASS
+SLAB = 512
+SUB = SLAB // P
+W_SLABS = FEATURES // SLAB
+AHEAD = 3
+
+FLOPS = 2 * TOKENS * FEATURES * FEATURES * 2 + 2 * TOKENS * KEYS * FEATURES
+
+
+def tile_siglipsdpaattention_pa_kernel(tc, x, Wq, bq, Wk, bk, out):
+    nc = tc.nc
+    with ExitStack() as ctx:
+        keep = ctx.enter_context(tc.tile_pool(name="keep", bufs=1))
+        stage = ctx.enter_context(tc.tile_pool(name="stage", bufs=3))
+        result = ctx.enter_context(tc.tile_pool(name="result", bufs=6))
+        psum = ctx.enter_context(tc.psum_pool(name="psum", bufs=8))
+        ctx.enter_context(tc.manual_schedule())
+
+        def bank(name):
+            return psum.tile([P, SLAB], F32, name=name, tag="bank")
+
+        x_slabs = x.flatten_outer_dims().rearrange(
+            "(s p r) k -> r p s k", p=P, r=WINDOW
+        )
+        wq_slabs = Wq.rearrange("(G p s) k -> G p s k", p=P, s=SUB)
+        wk_slabs = Wk.rearrange("(G p s) k -> G p s k", p=P, s=SUB)
+        out_blocks = out.flatten_outer_dims().rearrange(
+            "(s p r) m -> r s p m", p=P, r=WINDOW
+        )
+
+        x_codes = keep.tile([P, WINDOW, PASSES, SLAB], U32, align_bytes=64)
+        x_scales = keep.tile([P, WINDOW, PASSES, SLAB], U8, align_bytes=64)
+        wq_codes = keep.tile([P, W_SLABS, PASSES, SLAB], U32, align_bytes=64)
+        wq_scales = keep.tile([P, W_SLABS, PASSES, SLAB], U8, align_bytes=64)
+        wk_codes = keep.tile([P, W_SLABS, PASSES, SLAB], U32, align_bytes=64)
+        wk_scales = keep.tile([P, W_SLABS, PASSES, SLAB], U8, align_bytes=64)
+        q_codes = keep.tile([P, PASSES, WINDOW, SLAB], U32, align_bytes=64)
+        q_scales = keep.tile([P, PASSES, WINDOW, SLAB], U8, align_bytes=64)
+        k_codes = keep.tile([P, PASSES, KEYS], U32, align_bytes=64)
+        k_scales = keep.tile([P, PASSES, KEYS], U8, align_bytes=64)
+
+        slabs = (
+            [(wk_slabs[0], wk_codes[:, 0], wk_scales[:, 0])]
+            + [(x_slabs[r], x_codes[:, r], x_scales[:, r]) for r in range(WINDOW)]
+            + [(wq_slabs[0], wq_codes[:, 0], wq_scales[:, 0])]
+            + [(wk_slabs[1], wk_codes[:, 1], wk_scales[:, 1])]
+            + [(wq_slabs[1], wq_codes[:, 1], wq_scales[:, 1])]
+        )
+        raws = []
+        for n, slab in enumerate(slabs):
+            raw = keep.tile([P, SUB, FEATURES], BF16, name="raw%d" % n)
+            for half in range(2):
+                pair = slice(2 * half, 2 * half + 2)
+                nc.sync.dma_start(out=raw[:, pair, :], in_=slab[0][:, pair, :])
+            raws.append(raw)
+
+        bq_bf = keep.tile([P, W_SLABS, SUB], BF16)
+        bk_bf = keep.tile([P, W_SLABS, SUB], BF16)
+        nc.scalar.dma_start(
+            out=bq_bf[:], in_=bq.rearrange("(G p s) -> p G s", p=P, s=SUB)
+        )
+        nc.scalar.dma_start(
+            out=bk_bf[:], in_=bk.rearrange("(G p s) -> p G s", p=P, s=SUB)
+        )
+        bq_f32 = keep.tile([P, W_SLABS, SUB], F32)
+        bk_f32 = keep.tile([P, W_SLABS, SUB], F32)
+
+        identity = keep.tile([P, P], F32)
+        masks.make_identity(nc, identity[:])
+
+        def prepare_slab(n):
+            raw = raws[n]
+            codes, scales = slabs[n][1], slabs[n][2]
+            grouped = stage.tile([P, PASSES * SLAB * PACK], BF16, align_bytes=64)
+            grouped_words = grouped[:].bitcast(F32).rearrange(
+                "p (g c u) -> p g c u", g=PASSES, u=2
+            )
+            for half in range(2):
+                for g in range(PASSES):
+                    turned = bank("turned")
+                    for s in range(2):
+                        words = raw[:, 2 * half + s, :].bitcast(F32)
+                        for u in range(2):
+                            nc.tensor.transpose(
+                                turned[:, (2 * s + u) * P : (2 * s + u + 1) * P],
+                                words[:, (2 * g + u) * P : (2 * g + u + 1) * P],
+                                identity[:],
+                            )
+                    copy = nc.scalar.copy if g == 0 else nc.vector.tensor_copy
+                    copy(
+                        out=grouped_words[
+                            :, g, 2 * P * half : 2 * P * (half + 1), :
+                        ].rearrange("p (s c) u -> p s c u", s=2),
+                        in_=turned[:].rearrange("p (s u c) -> p s c u", s=2, u=2),
+                    )
+            for g in range(PASSES):
+                nc.vector.quantize_mx(
+                    out=codes[:, g, :].bitcast(FP8X4),
+                    scales=scales[:, g, :],
+                    in_=grouped[:, g * SLAB * PACK : (g + 1) * SLAB * PACK],
+                )
+
+        def project(acc, w_codes, w_scales, G, r, first, last):
+            for s in range(SUB):
+                cols = slice(s * P, (s + 1) * P)
+                for g in range(PASSES):
+                    nc.tensor.matmul_mx(
+                        out=acc[s][:],
+                        lhsT=w_codes[:, G, g, cols].bitcast(FP8X4),
+                        lhsT_scale=w_scales[:, G, g, cols],
+                        rhs=x_codes[:, r, g, :].bitcast(FP8X4),
+                        rhs_scale=x_scales[:, r, g, :],
+                        start=(first and g == 0),
+                        stop=(last and g == PASSES - 1),
+                    )
+
+        def finish(acc, scale, bias, codes, scales):
+            banks = stage.tile([P, SUB, SLAB], BF16)
+            for s in range(SUB):
+                nc.scalar.activation(
+                    out=banks[:, s, :],
+                    in_=acc[s][:],
+                    func=ACT.Identity,
+                    bias=bias[:, s : s + 1],
+                    scale=scale,
+                )
+            packed = stage.tile([P, SLAB, PACK], BF16, align_bytes=64)
+            nc.vector.tensor_copy(
+                out=packed[:].rearrange("p (c i) s -> p c s i", i=4),
+                in_=banks[:].rearrange("p s (c i) -> p c s i", i=4),
+            )
+            nc.vector.quantize_mx(
+                out=codes.bitcast(FP8X4),
+                scales=scales,
+                in_=packed[:].rearrange("p c s -> p (c s)"),
+            )
+
+        def query_unit(r, G):
+            acc = [bank("q_acc%d" % s) for s in range(SUB)]
+            project(acc, wq_codes, wq_scales, G, r, True, True)
+            finish(acc, 1.0, bq_f32[:, G, :], q_codes[:, G, r, :], q_scales[:, G, r, :])
+
+        def finish_keys(acc, G):
+            finish(
+                acc, 1.0 / WINDOW, bk_f32[:, G, :], k_codes[:, G, :], k_scales[:, G, :]
+            )
+
+        def score_unit(r):
+            acc = [bank("s_acc%d" % s) for s in range(SUB)]
+            for G in range(PASSES):
+                for s in range(SUB):
+                    cols = slice(s * P, (s + 1) * P)
+                    nc.tensor.matmul_mx(
+                        out=acc[s][:],
+                        lhsT=q_codes[:, G, r, cols].bitcast(FP8X4),
+                        lhsT_scale=q_scales[:, G, r, cols],
+                        rhs=k_codes[:, G, :].bitcast(FP8X4),
+                        rhs_scale=k_scales[:, G, :],
+                        start=(G == 0),
+                        stop=(G == PASSES - 1),
+                    )
+            for s in range(SUB):
+                logits = result.tile([P, KEYS], F32)
+                if s % 2 == 0:
+                    nc.vector.tensor_scalar(
+                        out=logits[:],
+                        in0=acc[s][:],
+                        scalar1=1.0 / math.sqrt(FEATURES),
+                        scalar2=math.log(WINDOW),
+                        op0=ALU.mult,
+                        op1=ALU.add,
+                    )
+                else:
+                    nc.scalar.activation(
+                        out=logits[:],
+                        in_=acc[s][:],
+                        func=ACT.Copy,
+                        bias=math.log(WINDOW),
+                        scale=1.0 / math.sqrt(FEATURES),
+                    )
+                nc.sync.dma_start(out=out_blocks[r, s], in_=logits[:])
+
+        for n in range(AHEAD):
+            prepare_slab(n)
+        nc.vector.tensor_copy(out=bq_f32[:], in_=bq_bf[:])
+        nc.vector.tensor_copy(out=bk_f32[:], in_=bk_bf[:])
+
+        k_acc = [bank("k_acc%d" % s) for s in range(SUB)]
+        for r in range(WINDOW):
+            project(k_acc, wk_codes, wk_scales, 0, r, r == 0, r == WINDOW - 1)
+            if r == WINDOW - 1:
+                finish_keys(k_acc, 0)
+            prepare_slab(AHEAD + r)
+
+        k_acc = [bank("k_acc%d" % s) for s in range(SUB)]
+        for r in range(WINDOW):
+            query_unit(r, 0)
+            if AHEAD + WINDOW + r < len(slabs):
+                prepare_slab(AHEAD + WINDOW + r)
+            project(k_acc, wk_codes, wk_scales, 1, r, r == 0, r == WINDOW - 1)
+        finish_keys(k_acc, 1)
+
+        for r in range(WINDOW):
+            query_unit(r, 1)
+            if r > 0:
+                score_unit(r - 1)
+        score_unit(WINDOW - 1)

@@ -35,7 +35,6 @@ def tile_siglipsdpaattention_pa_kernel(tc, x, Wq, bq, Wk, bk, out):
         stage = ctx.enter_context(tc.tile_pool(name="stage", bufs=3))
         result = ctx.enter_context(tc.tile_pool(name="result", bufs=6))
         psum = ctx.enter_context(tc.psum_pool(name="psum", bufs=8))
-        ctx.enter_context(tc.manual_schedule())
 
         def bank(name):
             return psum.tile([P, SLAB], F32, name=name, tag="bank")

@@ -22,6 +22,8 @@ KEYS = TOKENS // WINDOW
 PASSES = FEATURES // K_PASS
 SLAB = 512
 SUB = SLAB // P
+HALVES = 2
+HALF = SLAB // HALVES
 W_SLABS = FEATURES // SLAB
 AHEAD = 3
 
@@ -32,7 +34,7 @@ def tile_siglipsdpaattention_pa_kernel(tc, x, Wq, bq, Wk, bk, out):
     nc = tc.nc
     with ExitStack() as ctx:
         keep = ctx.enter_context(tc.tile_pool(name="keep", bufs=1))
-        stage = ctx.enter_context(tc.tile_pool(name="stage", bufs=3))
+        stage = ctx.enter_context(tc.tile_pool(name="stage", bufs=4))
         result = ctx.enter_context(tc.tile_pool(name="result", bufs=6))
         psum = ctx.enter_context(tc.psum_pool(name="psum", bufs=8))
 
@@ -60,28 +62,34 @@ def tile_siglipsdpaattention_pa_kernel(tc, x, Wq, bq, Wk, bk, out):
         k_scales = keep.tile([P, PASSES, KEYS], U8, align_bytes=64)
 
         slabs = (
-            [(wk_slabs[0], wk_codes[:, 0], wk_scales[:, 0])]
-            + [(x_slabs[r], x_codes[:, r], x_scales[:, r]) for r in range(WINDOW)]
+            [(x_slabs[0], x_codes[:, 0], x_scales[:, 0])]
+            + [(wk_slabs[0], wk_codes[:, 0], wk_scales[:, 0])]
+            + [(x_slabs[r], x_codes[:, r], x_scales[:, r]) for r in range(1, WINDOW)]
             + [(wq_slabs[0], wq_codes[:, 0], wq_scales[:, 0])]
             + [(wk_slabs[1], wk_codes[:, 1], wk_scales[:, 1])]
             + [(wq_slabs[1], wq_codes[:, 1], wq_scales[:, 1])]
         )
         raws = []
-        for n, slab in enumerate(slabs):
+
+        def load_slab(n):
             raw = keep.tile([P, SUB, FEATURES], BF16, name="raw%d" % n)
-            for half in range(2):
+            for half in range(HALVES):
                 pair = slice(2 * half, 2 * half + 2)
-                nc.sync.dma_start(out=raw[:, pair, :], in_=slab[0][:, pair, :])
+                nc.sync.dma_start(out=raw[:, pair, :], in_=slabs[n][0][:, pair, :])
             raws.append(raw)
 
+        for n in range(AHEAD):
+            load_slab(n)
         bq_bf = keep.tile([P, W_SLABS, SUB], BF16)
         bk_bf = keep.tile([P, W_SLABS, SUB], BF16)
-        nc.scalar.dma_start(
-            out=bq_bf[:], in_=bq.rearrange("(G p s) -> p G s", p=P, s=SUB)
-        )
-        nc.scalar.dma_start(
+        nc.sync.dma_start(
             out=bk_bf[:], in_=bk.rearrange("(G p s) -> p G s", p=P, s=SUB)
         )
+        nc.sync.dma_start(
+            out=bq_bf[:], in_=bq.rearrange("(G p s) -> p G s", p=P, s=SUB)
+        )
+        for n in range(AHEAD, len(slabs)):
+            load_slab(n)
         bq_f32 = keep.tile([P, W_SLABS, SUB], F32)
         bk_f32 = keep.tile([P, W_SLABS, SUB], F32)
 
@@ -91,11 +99,9 @@ def tile_siglipsdpaattention_pa_kernel(tc, x, Wq, bq, Wk, bk, out):
         def prepare_slab(n):
             raw = raws[n]
             codes, scales = slabs[n][1], slabs[n][2]
-            grouped = stage.tile([P, PASSES * SLAB * PACK], BF16, align_bytes=64)
-            grouped_words = grouped[:].bitcast(F32).rearrange(
-                "p (g c u) -> p g c u", g=PASSES, u=2
-            )
-            for half in range(2):
+            for half in range(HALVES):
+                cols = slice(half * HALF, (half + 1) * HALF)
+                grouped = stage.tile([P, PASSES, HALF * PACK], BF16, align_bytes=64)
                 for g in range(PASSES):
                     turned = bank("turned")
                     for s in range(2):
@@ -108,17 +114,17 @@ def tile_siglipsdpaattention_pa_kernel(tc, x, Wq, bq, Wk, bk, out):
                             )
                     copy = nc.scalar.copy if g == 0 else nc.vector.tensor_copy
                     copy(
-                        out=grouped_words[
-                            :, g, 2 * P * half : 2 * P * (half + 1), :
-                        ].rearrange("p (s c) u -> p s c u", s=2),
+                        out=grouped[:, g, :]
+                        .bitcast(F32)
+                        .rearrange("p (s c u) -> p s c u", s=2, u=2),
                         in_=turned[:].rearrange("p (s u c) -> p s c u", s=2, u=2),
                     )
-            for g in range(PASSES):
-                nc.vector.quantize_mx(
-                    out=codes[:, g, :].bitcast(FP8X4),
-                    scales=scales[:, g, :],
-                    in_=grouped[:, g * SLAB * PACK : (g + 1) * SLAB * PACK],
-                )
+                for g in range(PASSES):
+                    nc.vector.quantize_mx(
+                        out=codes[:, g, cols].bitcast(FP8X4),
+                        scales=scales[:, g, cols],
+                        in_=grouped[:, g, :],
+                    )
 
         def project(acc, w_codes, w_scales, G, r, first, last):
             for s in range(SUB):

import math
from contextlib import ExitStack

import concourse.masks as masks
import concourse.mybir as mybir

BF16 = mybir.dt.bfloat16
F32 = mybir.dt.float32
U32 = mybir.dt.uint32
U8 = mybir.dt.uint8
FP8X4 = mybir.dt.float8_e4m3fn_x4
ACT = mybir.ActivationFunctionType
ALU = mybir.AluOpType

P = 128
PACK = 4
K_PASS = P * PACK
TOKENS = 2048
FEATURES = 1024
WINDOW = 4
KEYS = TOKENS // WINDOW
PASSES = FEATURES // K_PASS
SLAB = 512
SUB = SLAB // P
HALVES = 2
HALF = SLAB // HALVES
W_SLABS = FEATURES // SLAB
AHEAD = 3

FLOPS = 2 * TOKENS * FEATURES * FEATURES * 2 + 2 * TOKENS * KEYS * FEATURES


def tile_siglipsdpaattention_pa_kernel(tc, x, Wq, bq, Wk, bk, out):
    nc = tc.nc
    with ExitStack() as ctx:
        keep = ctx.enter_context(tc.tile_pool(name="keep", bufs=1))
        stage = ctx.enter_context(tc.tile_pool(name="stage", bufs=4))
        result = ctx.enter_context(tc.tile_pool(name="result", bufs=6))
        psum = ctx.enter_context(tc.psum_pool(name="psum", bufs=8))

        def bank(name):
            return psum.tile([P, SLAB], F32, name=name, tag="bank")

        x_slabs = x.flatten_outer_dims().rearrange(
            "(s p r) k -> r p s k", p=P, r=WINDOW
        )
        wq_slabs = Wq.rearrange("(G p s) k -> G p s k", p=P, s=SUB)
        wk_slabs = Wk.rearrange("(G p s) k -> G p s k", p=P, s=SUB)
        out_blocks = out.flatten_outer_dims().rearrange(
            "(s p r) m -> r s p m", p=P, r=WINDOW
        )

        x_codes = keep.tile([P, WINDOW, PASSES, SLAB], U32, align_bytes=64)
        x_scales = keep.tile([P, WINDOW, PASSES, SLAB], U8, align_bytes=64)
        wq_codes = keep.tile([P, W_SLABS, PASSES, SLAB], U32, align_bytes=64)
        wq_scales = keep.tile([P, W_SLABS, PASSES, SLAB], U8, align_bytes=64)
        wk_codes = keep.tile([P, W_SLABS, PASSES, SLAB], U32, align_bytes=64)
        wk_scales = keep.tile([P, W_SLABS, PASSES, SLAB], U8, align_bytes=64)
        q_codes = keep.tile([P, PASSES, WINDOW, SLAB], U32, align_bytes=64)
        q_scales = keep.tile([P, PASSES, WINDOW, SLAB], U8, align_bytes=64)
        k_codes = keep.tile([P, PASSES, KEYS], U32, align_bytes=64)
        k_scales = keep.tile([P, PASSES, KEYS], U8, align_bytes=64)

        slabs = (
            [(x_slabs[0], x_codes[:, 0], x_scales[:, 0])]
            + [(wk_slabs[0], wk_codes[:, 0], wk_scales[:, 0])]
            + [(x_slabs[r], x_codes[:, r], x_scales[:, r]) for r in range(1, WINDOW)]
            + [(wq_slabs[0], wq_codes[:, 0], wq_scales[:, 0])]
            + [(wk_slabs[1], wk_codes[:, 1], wk_scales[:, 1])]
            + [(wq_slabs[1], wq_codes[:, 1], wq_scales[:, 1])]
        )
        raws = []

        def load_slab(n):
            raw = keep.tile([P, SUB, FEATURES], BF16, name="raw%d" % n)
            for half in range(HALVES):
                pair = slice(2 * half, 2 * half + 2)
                nc.sync.dma_start(out=raw[:, pair, :], in_=slabs[n][0][:, pair, :])
            raws.append(raw)

        for n in range(AHEAD):
            load_slab(n)
        bq_bf = keep.tile([P, W_SLABS, SUB], BF16)
        bk_bf = keep.tile([P, W_SLABS, SUB], BF16)
        nc.sync.dma_start(
            out=bk_bf[:], in_=bk.rearrange("(G p s) -> p G s", p=P, s=SUB)
        )
        nc.sync.dma_start(
            out=bq_bf[:], in_=bq.rearrange("(G p s) -> p G s", p=P, s=SUB)
        )
        for n in range(AHEAD, len(slabs)):
            load_slab(n)
        bq_f32 = keep.tile([P, W_SLABS, SUB], F32)
        bk_f32 = keep.tile([P, W_SLABS, SUB], F32)

        identity = keep.tile([P, P], F32)
        masks.make_identity(nc, identity[:])

        def prepare_slab(n):
            raw = raws[n]
            codes, scales = slabs[n][1], slabs[n][2]
            for half in range(HALVES):
                cols = slice(half * HALF, (half + 1) * HALF)
                grouped = stage.tile([P, PASSES, HALF * PACK], BF16, align_bytes=64)
                for g in range(PASSES):
                    turned = bank("turned")
                    for s in range(2):
                        words = raw[:, 2 * half + s, :].bitcast(F32)
                        for u in range(2):
                            nc.tensor.transpose(
                                turned[:, (2 * s + u) * P : (2 * s + u + 1) * P],
                                words[:, (2 * g + u) * P : (2 * g + u + 1) * P],
                                identity[:],
                            )
                    copy = nc.scalar.copy if g == 0 else nc.vector.tensor_copy
                    copy(
                        out=grouped[:, g, :]
                        .bitcast(F32)
                        .rearrange("p (s c u) -> p s c u", s=2, u=2),
                        in_=turned[:].rearrange("p (s u c) -> p s c u", s=2, u=2),
                    )
                for g in range(PASSES):
                    nc.vector.quantize_mx(
                        out=codes[:, g, cols].bitcast(FP8X4),
                        scales=scales[:, g, cols],
                        in_=grouped[:, g, :],
                    )

        def project(acc, w_codes, w_scales, G, r, first, last):
            for s in range(SUB):
                cols = slice(s * P, (s + 1) * P)
                for g in range(PASSES):
                    nc.tensor.matmul_mx(
                        out=acc[s][:],
                        lhsT=w_codes[:, G, g, cols].bitcast(FP8X4),
                        lhsT_scale=w_scales[:, G, g, cols],
                        rhs=x_codes[:, r, g, :].bitcast(FP8X4),
                        rhs_scale=x_scales[:, r, g, :],
                        start=(first and g == 0),
                        stop=(last and g == PASSES - 1),
                    )

        def finish(acc, scale, bias, codes, scales):
            banks = stage.tile([P, SUB, SLAB], BF16)
            for s in range(SUB):
                nc.scalar.activation(
                    out=banks[:, s, :],
                    in_=acc[s][:],
                    func=ACT.Identity,
                    bias=bias[:, s : s + 1],
                    scale=scale,
                )
            packed = stage.tile([P, SLAB, PACK], BF16, align_bytes=64)
            nc.vector.tensor_copy(
                out=packed[:].rearrange("p (c i) s -> p c s i", i=4),
                in_=banks[:].rearrange("p s (c i) -> p c s i", i=4),
            )
            nc.vector.quantize_mx(
                out=codes.bitcast(FP8X4),
                scales=scales,
                in_=packed[:].rearrange("p c s -> p (c s)"),
            )

        def query_unit(r, G):
            acc = [bank("q_acc%d" % s) for s in range(SUB)]
            project(acc, wq_codes, wq_scales, G, r, True, True)
            finish(acc, 1.0, bq_f32[:, G, :], q_codes[:, G, r, :], q_scales[:, G, r, :])

        def finish_keys(acc, G):
            finish(
                acc, 1.0 / WINDOW, bk_f32[:, G, :], k_codes[:, G, :], k_scales[:, G, :]
            )

        def score_unit(r):
            acc = [bank("s_acc%d" % s) for s in range(SUB)]
            for G in range(PASSES):
                for s in range(SUB):
                    cols = slice(s * P, (s + 1) * P)
                    nc.tensor.matmul_mx(
                        out=acc[s][:],
                        lhsT=q_codes[:, G, r, cols].bitcast(FP8X4),
                        lhsT_scale=q_scales[:, G, r, cols],
                        rhs=k_codes[:, G, :].bitcast(FP8X4),
                        rhs_scale=k_scales[:, G, :],
                        start=(G == 0),
                        stop=(G == PASSES - 1),
                    )
            for s in range(SUB):
                logits = result.tile([P, KEYS], F32)
                if s % 2 == 0:
                    nc.vector.tensor_scalar(
                        out=logits[:],
                        in0=acc[s][:],
                        scalar1=1.0 / math.sqrt(FEATURES),
                        scalar2=math.log(WINDOW),
                        op0=ALU.mult,
                        op1=ALU.add,
                    )
                else:
                    nc.scalar.activation(
                        out=logits[:],
                        in_=acc[s][:],
                        func=ACT.Copy,
                        bias=math.log(WINDOW),
                        scale=1.0 / math.sqrt(FEATURES),
                    )
                nc.sync.dma_start(out=out_blocks[r, s], in_=logits[:])

        for n in range(AHEAD):
            prepare_slab(n)
        nc.vector.tensor_copy(out=bq_f32[:], in_=bq_bf[:])
        nc.vector.tensor_copy(out=bk_f32[:], in_=bk_bf[:])

        k_acc = [bank("k_acc%d" % s) for s in range(SUB)]
        for r in range(WINDOW):
            project(k_acc, wk_codes, wk_scales, 0, r, r == 0, r == WINDOW - 1)
            if r == WINDOW - 1:
                finish_keys(k_acc, 0)
            prepare_slab(AHEAD + r)

        k_acc = [bank("k_acc%d" % s) for s in range(SUB)]
        for r in range(WINDOW):
            query_unit(r, 0)
            if AHEAD + WINDOW + r < len(slabs):
                prepare_slab(AHEAD + WINDOW + r)
            project(k_acc, wk_codes, wk_scales, 1, r, r == 0, r == WINDOW - 1)
        finish_keys(k_acc, 1)

        for r in range(WINDOW):
            query_unit(r, 1)
            if r > 0:
                score_unit(r - 1)
        score_unit(WINDOW - 1)
